import numpy as np
import ml_dtypes


def mxq(x, axis, fmt="e4m3"):
    dtype, down = {"e4m3": (ml_dtypes.float8_e4m3fn, 7), "e5m2": (ml_dtypes.float8_e5m2, 14)}[fmt]
    v = np.moveaxis(np.asarray(x, np.float32).astype(ml_dtypes.bfloat16).astype(np.float64), axis, -1)
    blocks = v.reshape(v.shape[:-1] + (-1, 32))
    amax = np.abs(blocks).max(-1, keepdims=True)
    byte = np.maximum(np.where(amax > 0, np.frexp(amax)[1] - 1 + 127, 0) - down, 1)
    scale = np.exp2(byte - 127.0)
    codes = (blocks / scale).astype(np.float32).astype(dtype).astype(np.float64)
    return np.moveaxis((codes * scale).reshape(v.shape), -1, axis)


BF16 = ml_dtypes.bfloat16


def bf(x):
    return np.asarray(x, np.float32).astype(BF16)


def f64(x):
    return np.asarray(x).astype(np.float64)


Q, K, D = 8192, 512, 1024
EPS = 1e-6


def setup_inputs():
    p = np.random.standard_normal((K, D)) * 5.6 / np.sqrt(D)
    own = np.random.randint(0, K, Q)
    r = 1.0 + 2.0 * np.random.random_sample((Q, 1))
    q = p[own] + np.random.standard_normal((Q, D)) * r / np.sqrt(D)
    return {"class_prototypes": bf(p), "query_features": bf(q)}


def reference(class_prototypes, query_features):
    p = f64(class_prototypes)
    q = f64(query_features)
    d = q.shape[1]
    q_sq = np.sum(q * q, axis=1)
    p_sq = np.sum(p * p, axis=1)
    cross = mxq(q, 1, "e4m3") @ mxq(p, 1, "e4m3").T
    lin = 2.0 * EPS * (np.sum(q, axis=1)[:, None] - np.sum(p, axis=1)[None, :])
    sq = q_sq[:, None] + p_sq[None, :] - 2.0 * cross + lin + d * EPS * EPS
    dist = np.sqrt(np.maximum(sq, 0.0))
    post = np.exp(-dist)
    post = post / np.sum(post, axis=1, keepdims=True)
    c = np.max(post, axis=1)
    h = -np.sum(post * np.log(post), axis=1)
    return (post, c, h)

@@ -1,0 +1,281 @@
+from contextlib import ExitStack
+
+import concourse.bass as bass
+import concourse.mybir as mybir
+import concourse.tile as tile
+from concourse.masks import make_identity
+
+F32 = mybir.dt.float32
+BF16 = mybir.dt.bfloat16
+U32 = mybir.dt.uint32
+U8 = mybir.dt.uint8
+FP8X4 = mybir.dt.float8_e4m3fn_x4
+ACT = mybir.ActivationFunctionType
+ALU = mybir.AluOpType
+
+P = 128
+NQ, NK, D = 8192, 512, 1024
+EPS = 1e-6
+NT = NQ // P
+UT = 2
+NU = NT // UT
+CT = 4
+NCH = NT // CT
+W = D // 2
+FLOPS = 2 * NQ * NK * D
+
+
+def c_on_scalar(t):
+    return t % 3 == 0 and t >= 6
+
+
+def n_on_scalar(t):
+    return t % 2 == 1
+
+
+def tile_modalityspecificposterior_t_kernel(tc, class_prototypes, query_features, out_0, out_1, out_2):
+    nc = tc.nc
+    qv = query_features.rearrange("(p t) d -> p t d", t=NT)
+    ov = out_0.rearrange("(p t) k -> p t k", t=NT)
+    pv = class_prototypes.rearrange("(c r) d -> r c d", r=P)
+
+    with ExitStack() as ctx:
+        ctx.enter_context(tc.manual_schedule())
+        const = ctx.enter_context(tc.tile_pool(name="const", bufs=1))
+        keep = ctx.enter_context(tc.tile_pool(name="keep", bufs=1))
+        qpool = ctx.enter_context(tc.tile_pool(name="qpool", bufs=3))
+        gpool = ctx.enter_context(tc.tile_pool(name="gpool", bufs=3))
+        epool = ctx.enter_context(tc.tile_pool(name="epool", bufs=8))
+        ps_t = ctx.enter_context(tc.psum_pool(name="ps_t", bufs=4))
+        ps_a = ctx.enter_context(tc.psum_pool(name="ps_a", bufs=4))
+
+        ident = const.tile([P, P], F32, name="ident")
+        make_identity(nc, ident[:])
+        eps_pos = const.tile([P, 1], F32, name="eps_pos")
+        eps_neg = const.tile([P, 1], F32, name="eps_neg")
+        warm = const.tile([P, 1], F32, name="warm")
+        nc.vector.memset(eps_pos[:], EPS)
+        nc.vector.memset(eps_neg[:], -EPS)
+        nc.scalar.activation(out=warm[:], in_=eps_pos[:], func=ACT.Sqrt)
+
+        qt = const.tile([P, NT], F32, name="qt")
+        um = const.tile([P, NT], F32, name="um")
+        dm2 = const.tile([P, NT], F32, name="dm2")
+        dmin = const.tile([P, NT], F32, name="dmin")
+        ssum = const.tile([P, NT], F32, name="ssum")
+        rs = const.tile([P, NT], F32, name="rs")
+        ed = const.tile([P, NT], F32, name="ed")
+        lns = const.tile([P, NT], F32, name="lns")
+        hh = const.tile([P, NT], F32, name="hh")
+        ps_sum = const.tile([P, 4], F32, name="ps_sum")
+        ps_fix = const.tile([P, 4], F32, name="ps_fix")
+        junk = const.tile([P, D], BF16, name="junk")
+        pt = const.tile([P, NK], F32, name="pt")
+        rep = const.tile([P, 4, P], F32, name="rep")
+
+        p_sb = const.tile([P, 4, D], BF16, name="p_sb")
+        gp = const.tile([P, 2 * NK * 2], F32, name="gp", align_bytes=64)
+        p_codes = const.tile([P, 2, NK], U32, name="p_codes", align_bytes=64)
+        p_scales = const.tile([P, 2, NK], U8, name="p_scales", align_bytes=64)
+
+        ds = [keep.tile([P, CT, NK], F32, name="ds%d" % c) for c in range(NCH)]
+
+        def ds_t(t):
+            return ds[t // CT][:, t % CT, :]
+
+        for c in range(4):
+            nc.sync.dma_start(out=p_sb[:, c, :], in_=pv[:, c, :])
+        qch = {}
+
+        def load(c):
+            qc = qpool.tile([P, CT, D], BF16, name="qc")
+            nc.sync.dma_start(out=qc[:], in_=qv[:, c * CT : (c + 1) * CT, :])
+            qch[c] = qc
+
+        load(0)
+        load(1)
+        load(2)
+
+        gp_v = gp[:].rearrange("p (g k u) -> p g k u", g=2, u=2)
+        p_w = p_sb[:].bitcast(F32)
+        for c in range(4):
+            xt = ps_t.tile([P, 4, P], F32, name="xt")
+            for b in range(4):
+                nc.tensor.transpose(xt[:, b, :], p_w[:, c, b * P : (b + 1) * P], ident[:])
+            nc.vector.tensor_copy(
+                out=gp_v[:, :, c * P : (c + 1) * P, :],
+                in_=xt[:].rearrange("p (g u) r -> p g r u", u=2),
+            )
+            nc.scalar.activation(
+                out=junk[:], in_=p_sb[:, c, :], func=ACT.Square, bias=eps_neg[:], scale=1.0,
+                accum_out=ps_sum[:, c : c + 1],
+            )
+        gp_b = gp[:].bitcast(BF16)
+        for g in range(2):
+            nc.vector.quantize_mx(
+                out=p_codes[:, g, :].bitcast(FP8X4),
+                scales=p_scales[:, g, :],
+                in_=gp_b[:, g * 4 * NK : (g + 1) * 4 * NK],
+            )
+
+        def build_pt():
+            nc.vector.tensor_scalar_add(out=ps_fix[:], in0=ps_sum[:], scalar1=-(D * EPS * EPS))
+            ptp = ps_a.tile([P, NK], F32, name="acc")
+            for c in range(4):
+                nc.vector.tensor_scalar(
+                    out=rep[:, c, :], in0=ident[:], scalar1=0.0, scalar2=ps_fix[:, c : c + 1],
+                    op0=ALU.mult, op1=ALU.add,
+                )
+            for c in range(4):
+                nc.tensor.transpose(ptp[:, c * P : (c + 1) * P], rep[:, c, :], ident[:])
+            nc.vector.tensor_copy(out=pt[:], in_=ptp[:])
+
+        xts = {}
+        grp = {}
+        cod = {}
+        accs = {}
+
+        def do_T(u):
+            for j in range(UT):
+                t = u * UT + j
+                qw = qch[t // CT][:].bitcast(F32)
+                xt = ps_t.tile([P, 4, P], F32, name="xt")
+                for b in range(4):
+                    nc.tensor.transpose(xt[:, b, :], qw[:, t % CT, b * P : (b + 1) * P], ident[:])
+                xts[t] = xt
+
+        def do_C(u):
+            g = gpool.tile([P, UT * W], F32, name="grouped", align_bytes=64)
+            grp[u] = g
+            for j in range(UT):
+                t = u * UT + j
+                dst = g[:, j * W : (j + 1) * W].rearrange("p (g q u) -> p g q u", g=2, u=2)
+                src = xts[t][:].rearrange("p (g u) q -> p g q u", u=2)
+                if c_on_scalar(t):
+                    nc.scalar.copy(out=dst, in_=src)
+                else:
+                    nc.vector.tensor_copy(out=dst, in_=src)
+
+        def do_Z(u):
+            codes = gpool.tile([P, UT * 2 * P], U32, name="codes", align_bytes=64)
+            scales = gpool.tile([P, UT * 2 * P], U8, name="scales", align_bytes=64)
+            nc.vector.quantize_mx(out=codes[:].bitcast(FP8X4), scales=scales[:], in_=grp[u][:].bitcast(BF16))
+            cod[u] = (codes, scales)
+
+        def do_M(u):
+            codes, scales = cod[u]
+            for j in range(UT):
+                t = u * UT + j
+                acc = ps_a.tile([P, NK], F32, name="acc")
+                for g in range(2):
+                    o = (j * 2 + g) * P
+                    nc.tensor.matmul_mx(
+                        out=acc[:],
+                        lhsT=codes[:, o : o + P].bitcast(FP8X4),
+                        lhsT_scale=scales[:, o : o + P],
+                        rhs=p_codes[:, g, :].bitcast(FP8X4),
+                        rhs_scale=p_scales[:, g, :],
+                        start=(g == 0),
+                        stop=(g == 1),
+                    )
+                accs[t] = acc
+
+        def do_Q(u):
+            for j in range(UT):
+                t = u * UT + j
+                nc.scalar.activation(
+                    out=junk[:], in_=qch[t // CT][:, t % CT, :], func=ACT.Square, bias=eps_pos[:], scale=1.0,
+                    accum_out=qt[:, t : t + 1],
+                )
+
+        def do_AB(u):
+            for j in range(UT):
+                t = u * UT + j
+                nc.vector.scalar_tensor_tensor(
+                    out=ds_t(t), in0=accs[t][:], scalar=2.0, in1=pt[:], op0=ALU.mult, op1=ALU.subtract,
+                )
+            for j in range(UT):
+                t = u * UT + j
+                nc.vector.tensor_scalar(
+                    out=ds_t(t), in0=ds_t(t), scalar1=qt[:, t : t + 1], scalar2=None,
+                    op0=ALU.min, op1=ALU.max, accum_out=um[:, t : t + 1],
+                )
+
+        def do_R(u):
+            for j in range(UT):
+                t = u * UT + j
+                nc.scalar.activation(
+                    out=ds_t(t), in_=ds_t(t), func=ACT.Sqrt, bias=qt[:, t : t + 1], scale=-1.0,
+                )
+
+        for s in range(-2, NU + 1):
+            if (s + 4) % 2 == 0 and 3 <= (s + 4) // 2 < NCH:
+                load((s + 4) // 2)
+            if 0 <= s + 2 < NU:
+                do_T(s + 2)
+            if 0 <= s + 1 < NU:
+                do_Z(s + 1)
+                do_M(s + 1)
+            if 0 <= s + 2 < NU:
+                do_C(s + 2)
+            if 0 <= s + 1 < NU:
+                do_Q(s + 1)
+            if s == -1:
+                build_pt()
+            if 0 <= s < NU:
+                do_AB(s)
+            if 0 <= s - 1 < NU:
+                do_R(s - 1)
+
+        nc.vector.tensor_sub(out=dm2[:], in0=qt[:], in1=um[:])
+        nc.scalar.activation(out=dmin[:], in_=dm2[:], func=ACT.Sqrt)
+
+        es = {}
+
+        def do_E(u):
+            for j in range(UT):
+                t = u * UT + j
+                e = epool.tile([P, NK], F32, name="e")
+                nc.scalar.activation(
+                    out=e[:], in_=ds_t(t), func=ACT.Exp, bias=dmin[:, t : t + 1], scale=-1.0,
+                    accum_out=ssum[:, t : t + 1],
+                )
+                es[t] = e
+
+        def do_H(u):
+            t0 = u * UT
+            nc.vector.reciprocal(out=rs[:, t0 : t0 + UT], in_=ssum[:, t0 : t0 + UT])
+            for j in range(UT):
+                t = t0 + j
+                nc.vector.scalar_tensor_tensor(
+                    out=ds_t(t), in0=ds_t(t), scalar=dmin[:, t : t + 1], in1=es[t][:],
+                    op0=ALU.subtract, op1=ALU.mult, accum_out=ed[:, t : t + 1],
+                )
+
+        def do_N(u, on_scalar):
+            for j in range(UT):
+                t = u * UT + j
+                if n_on_scalar(t) != on_scalar:
+                    continue
+                if on_scalar:
+                    nc.scalar.activation(out=ds_t(t), in_=es[t][:], func=ACT.Copy, scale=rs[:, t : t + 1])
+                else:
+                    nc.vector.tensor_scalar_mul(out=ds_t(t), in0=es[t][:], scalar1=rs[:, t : t + 1])
+
+        for s in range(-1, NU + 1):
+            if 0 <= s + 1 < NU:
+                do_E(s + 1)
+            if 0 <= s < NU:
+                do_H(s)
+                do_N(s, False)
+            if 0 <= s - 1 < NU:
+                do_N(s - 1, True)
+                if (s - 1) % 2 == 1:
+                    c = (s - 1) // 2
+                    nc.sync.dma_start(out=ov[:, c * CT : (c + 1) * CT, :], in_=ds[c][:])
+
+        nc.sync.dma_start(out=out_1.rearrange("(p t) -> p t", t=NT), in_=rs[:])
+        nc.scalar.activation(out=lns[:], in_=ssum[:], func=ACT.Ln)
+        nc.vector.tensor_mul(out=hh[:], in0=ed[:], in1=rs[:])
+        nc.vector.tensor_add(out=hh[:], in0=hh[:], in1=lns[:])
+        nc.sync.dma_start(out=out_2.rearrange("(p t) -> p t", t=NT), in_=hh[:])

@@ -22,11 +22,18 @@ NU = NT // UT
 CT = 4
 NCH = NT // CT
 W = D // 2
+QS = 136
+NB = UT * 2
+C0 = D * EPS * EPS / (1.0 + 2.0 * EPS)
 FLOPS = 2 * NQ * NK * D
 
 
 def c_on_scalar(t):
     return t % 3 == 0 and t >= 6
+
+
+def diag(t):
+    return t % 8 in (1, 4, 6)
 
 
 def n_on_scalar(t):
@@ -45,12 +52,21 @@ def tile_modalityspecificposterior_t_kernel(tc, class_prototypes, query_features
         keep = ctx.enter_context(tc.tile_pool(name="keep", bufs=1))
         qpool = ctx.enter_context(tc.tile_pool(name="qpool", bufs=3))
         gpool = ctx.enter_context(tc.tile_pool(name="gpool", bufs=3))
+        gfix = ctx.enter_context(tc.tile_pool(name="gfix", bufs=1))
         epool = ctx.enter_context(tc.tile_pool(name="epool", bufs=8))
-        ps_t = ctx.enter_context(tc.psum_pool(name="ps_t", bufs=4))
+        ps_t = ctx.enter_context(tc.psum_pool(name="ps_t", bufs=3))
+        ps_d = ctx.enter_context(tc.psum_pool(name="ps_d", bufs=1))
         ps_a = ctx.enter_context(tc.psum_pool(name="ps_a", bufs=4))
 
-        ident = const.tile([P, P], F32, name="ident")
-        make_identity(nc, ident[:])
+        mask = const.tile([P, P + 4], F32, name="mask")
+        ident = mask[:, 0:P]
+        make_identity(nc, ident)
+        nc.vector.memset(mask[:, P : P + 1], 2.0 * EPS)
+        junkd = const.tile([P, P + 4], F32, name="junkd")
+        gbuf = [gfix.tile([P, NB * QS * 2], F32, name="grp%d" % i, align_bytes=64) for i in range(3)]
+        for i in range(3):
+            ones = gbuf[i][:].bitcast(BF16).rearrange("p (b s t) -> p b s t", b=NB, t=4)
+            nc.vector.memset(ones[:, :, P, :], 1.0)
         eps_pos = const.tile([P, 1], F32, name="eps_pos")
         eps_neg = const.tile([P, 1], F32, name="eps_neg")
         warm = const.tile([P, 1], F32, name="warm")
@@ -59,6 +75,10 @@ def tile_modalityspecificposterior_t_kernel(tc, class_prototypes, query_features
         nc.scalar.activation(out=warm[:], in_=eps_pos[:], func=ACT.Sqrt)
 
         qt = const.tile([P, NT], F32, name="qt")
+        qts = const.tile([P, NT], F32, name="qts")
+        qtv = const.tile([P, NT], F32, name="qtv")
+        nc.vector.memset(qts[:], 0.0)
+        nc.vector.memset(qtv[:], 0.0)
         um = const.tile([P, NT], F32, name="um")
         dm2 = const.tile([P, NT], F32, name="dm2")
         dmin = const.tile([P, NT], F32, name="dmin")
@@ -101,7 +121,7 @@ def tile_modalityspecificposterior_t_kernel(tc, class_prototypes, query_features
         for c in range(4):
             xt = ps_t.tile([P, 4, P], F32, name="xt")
             for b in range(4):
-                nc.tensor.transpose(xt[:, b, :], p_w[:, c, b * P : (b + 1) * P], ident[:])
+                nc.tensor.transpose(xt[:, b, :], p_w[:, c, b * P : (b + 1) * P], ident)
             nc.vector.tensor_copy(
                 out=gp_v[:, :, c * P : (c + 1) * P, :],
                 in_=xt[:].rearrange("p (g u) r -> p g r u", u=2),
@@ -123,11 +143,11 @@ def tile_modalityspecificposterior_t_kernel(tc, class_prototypes, query_features
             ptp = ps_a.tile([P, NK], F32, name="acc")
             for c in range(4):
                 nc.vector.tensor_scalar(
-                    out=rep[:, c, :], in0=ident[:], scalar1=0.0, scalar2=ps_fix[:, c : c + 1],
+                    out=rep[:, c, :], in0=ident, scalar1=0.0, scalar2=ps_fix[:, c : c + 1],
                     op0=ALU.mult, op1=ALU.add,
                 )
             for c in range(4):
-                nc.tensor.transpose(ptp[:, c * P : (c + 1) * P], rep[:, c, :], ident[:])
+                nc.tensor.transpose(ptp[:, c * P : (c + 1) * P], rep[:, c, :], ident)
             nc.vector.tensor_copy(out=pt[:], in_=ptp[:])
 
         xts = {}
@@ -141,15 +161,19 @@ def tile_modalityspecificposterior_t_kernel(tc, class_prototypes, query_features
                 qw = qch[t // CT][:].bitcast(F32)
                 xt = ps_t.tile([P, 4, P], F32, name="xt")
                 for b in range(4):
-                    nc.tensor.transpose(xt[:, b, :], qw[:, t % CT, b * P : (b + 1) * P], ident[:])
+                    nc.tensor.transpose(xt[:, b, :], qw[:, t % CT, b * P : (b + 1) * P], ident)
                 xts[t] = xt
 
+        def q_of(t):
+            return qtv[:, t : t + 1] if diag(t) else qts[:, t : t + 1]
+
         def do_C(u):
-            g = gpool.tile([P, UT * W], F32, name="grouped", align_bytes=64)
+            g = gbuf[u % 3]
             grp[u] = g
+            gv = g[:].rearrange("p (b s u) -> p b s u", b=NB, u=2)
             for j in range(UT):
                 t = u * UT + j
-                dst = g[:, j * W : (j + 1) * W].rearrange("p (g q u) -> p g q u", g=2, u=2)
+                dst = gv[:, 2 * j : 2 * j + 2, 0:P, :]
                 src = xts[t][:].rearrange("p (g u) q -> p g q u", u=2)
                 if c_on_scalar(t):
                     nc.scalar.copy(out=dst, in_=src)
@@ -159,8 +183,41 @@ def tile_modalityspecificposterior_t_kernel(tc, class_prototypes, query_features
         def do_Z(u):
             codes = gpool.tile([P, UT * 2 * P], U32, name="codes", align_bytes=64)
             scales = gpool.tile([P, UT * 2 * P], U8, name="scales", align_bytes=64)
-            nc.vector.quantize_mx(out=codes[:].bitcast(FP8X4), scales=scales[:], in_=grp[u][:].bitcast(BF16))
+            gb = grp[u][:].bitcast(BF16)
+            for b in range(NB):
+                nc.vector.quantize_mx(
+                    out=codes[:, b * P : (b + 1) * P].bitcast(FP8X4),
+                    scales=scales[:, b * P : (b + 1) * P],
+                    in_=gb[:, b * QS * 4 : b * QS * 4 + 4 * P],
+                )
             cod[u] = (codes, scales)
+
+        gds = {}
+
+        def do_D(u):
+            gb = grp[u][:].bitcast(BF16).rearrange("p (b s t) -> p b s t", b=NB, t=4)
+            for j in range(UT):
+                t = u * UT + j
+                if not diag(t):
+                    continue
+                gd = ps_d.tile([P, NK], F32, name="gd")
+                for i in range(8):
+                    b, v = 2 * j + i // 4, i % 4
+                    nc.tensor.matmul(
+                        out=gd[:, 0 : P + 1], lhsT=gb[:, b, 0:P, v], rhs=gb[:, b, 0 : P + 1, v],
+                        start=(i == 0), stop=(i == 7),
+                    )
+                gds[t] = gd
+
+        def do_X(u):
+            for j in range(UT):
+                t = u * UT + j
+                if not diag(t):
+                    continue
+                nc.vector.scalar_tensor_tensor(
+                    out=junkd[:, 0 : P + 1], in0=gds[t][:, 0 : P + 1], scalar=C0, in1=mask[:, 0 : P + 1],
+                    op0=ALU.add, op1=ALU.mult, accum_out=qtv[:, t : t + 1],
+                )
 
         def do_M(u):
             codes, scales = cod[u]
@@ -183,9 +240,11 @@ def tile_modalityspecificposterior_t_kernel(tc, class_prototypes, query_features
         def do_Q(u):
             for j in range(UT):
                 t = u * UT + j
+                if diag(t):
+                    continue
                 nc.scalar.activation(
                     out=junk[:], in_=qch[t // CT][:, t % CT, :], func=ACT.Square, bias=eps_pos[:], scale=1.0,
-                    accum_out=qt[:, t : t + 1],
+                    accum_out=qts[:, t : t + 1],
                 )
 
         def do_AB(u):
@@ -197,7 +256,7 @@ def tile_modalityspecificposterior_t_kernel(tc, class_prototypes, query_features
             for j in range(UT):
                 t = u * UT + j
                 nc.vector.tensor_scalar(
-                    out=ds_t(t), in0=ds_t(t), scalar1=qt[:, t : t + 1], scalar2=None,
+                    out=ds_t(t), in0=ds_t(t), scalar1=q_of(t), scalar2=None,
                     op0=ALU.min, op1=ALU.max, accum_out=um[:, t : t + 1],
                 )
 
@@ -205,7 +264,7 @@ def tile_modalityspecificposterior_t_kernel(tc, class_prototypes, query_features
             for j in range(UT):
                 t = u * UT + j
                 nc.scalar.activation(
-                    out=ds_t(t), in_=ds_t(t), func=ACT.Sqrt, bias=qt[:, t : t + 1], scale=-1.0,
+                    out=ds_t(t), in_=ds_t(t), func=ACT.Sqrt, bias=q_of(t), scale=-1.0,
                 )
 
         for s in range(-2, NU + 1):
@@ -216,6 +275,7 @@ def tile_modalityspecificposterior_t_kernel(tc, class_prototypes, query_features
             if 0 <= s + 1 < NU:
                 do_Z(s + 1)
                 do_M(s + 1)
+                do_D(s + 1)
             if 0 <= s + 2 < NU:
                 do_C(s + 2)
             if 0 <= s + 1 < NU:
@@ -224,9 +284,12 @@ def tile_modalityspecificposterior_t_kernel(tc, class_prototypes, query_features
                 build_pt()
             if 0 <= s < NU:
                 do_AB(s)
+            if 0 <= s + 1 < NU:
+                do_X(s + 1)
             if 0 <= s - 1 < NU:
                 do_R(s - 1)
 
+        nc.vector.tensor_add(out=qt[:], in0=qts[:], in1=qtv[:])
         nc.vector.tensor_sub(out=dm2[:], in0=qt[:], in1=um[:])
         nc.scalar.activation(out=dmin[:], in_=dm2[:], func=ACT.Sqrt)
 

@@ -29,15 +29,15 @@ FLOPS = 2 * NQ * NK * D
 
 
 def c_on_scalar(t):
-    return t % 3 == 0 and t >= 6
+    return t >= 4 and ((t // 2) % 4 != 3 or t % 2 == 0)
 
 
 def diag(t):
-    return t % 8 in (1, 4, 6)
+    return t % 2 == 1 and (t // 2) % 4 != 3
 
 
 def n_on_scalar(t):
-    return t % 2 == 1
+    return t % 8 in (1, 3, 5) and t < 60
 
 
 def tile_modalityspecificposterior_t_kernel(tc, class_prototypes, query_features, out_0, out_1, out_2):
@@ -107,12 +107,14 @@ def tile_modalityspecificposterior_t_kernel(tc, class_prototypes, query_features
             nc.sync.dma_start(out=p_sb[:, c, :], in_=pv[:, c, :])
         qch = {}
 
-        def load(c):
+        def load(c, pieces=1):
             qc = qpool.tile([P, CT, D], BF16, name="qc")
-            nc.sync.dma_start(out=qc[:], in_=qv[:, c * CT : (c + 1) * CT, :])
+            n = CT // pieces
+            for i in range(pieces):
+                nc.sync.dma_start(out=qc[:, i * n : (i + 1) * n, :], in_=qv[:, c * CT + i * n : c * CT + (i + 1) * n, :])
             qch[c] = qc
 
-        load(0)
+        load(0, 2)
         load(1)
         load(2)
 
@@ -138,47 +140,52 @@ def tile_modalityspecificposterior_t_kernel(tc, class_prototypes, query_features
                 in_=gp_b[:, g * 4 * NK : (g + 1) * 4 * NK],
             )
 
-        def build_pt():
+        def build_pt_rows():
             nc.vector.tensor_scalar_add(out=ps_fix[:], in0=ps_sum[:], scalar1=-(D * EPS * EPS))
-            ptp = ps_a.tile([P, NK], F32, name="acc")
             for c in range(4):
                 nc.vector.tensor_scalar(
                     out=rep[:, c, :], in0=ident, scalar1=0.0, scalar2=ps_fix[:, c : c + 1],
                     op0=ALU.mult, op1=ALU.add,
                 )
+            ptp = ps_a.tile([P, NK], F32, name="acc")
             for c in range(4):
                 nc.tensor.transpose(ptp[:, c * P : (c + 1) * P], rep[:, c, :], ident)
-            nc.vector.tensor_copy(out=pt[:], in_=ptp[:])
+            return ptp
 
         xts = {}
         grp = {}
         cod = {}
         accs = {}
 
+        def t_tile(t):
+            qw = qch[t // CT][:].bitcast(F32)
+            xt = ps_t.tile([P, 4, P], F32, name="xt")
+            for b in range(4):
+                nc.tensor.transpose(xt[:, b, :], qw[:, t % CT, b * P : (b + 1) * P], ident)
+            xts[t] = xt
+
         def do_T(u):
             for j in range(UT):
-                t = u * UT + j
-                qw = qch[t // CT][:].bitcast(F32)
-                xt = ps_t.tile([P, 4, P], F32, name="xt")
-                for b in range(4):
-                    nc.tensor.transpose(xt[:, b, :], qw[:, t % CT, b * P : (b + 1) * P], ident)
-                xts[t] = xt
+                t_tile(u * UT + j)
 
         def q_of(t):
             return qtv[:, t : t + 1] if diag(t) else qts[:, t : t + 1]
 
-        def do_C(u):
+        def c_tile(t):
+            u, j = t // UT, t % UT
             g = gbuf[u % 3]
             grp[u] = g
             gv = g[:].rearrange("p (b s u) -> p b s u", b=NB, u=2)
+            dst = gv[:, 2 * j : 2 * j + 2, 0:P, :]
+            src = xts[t][:].rearrange("p (g u) q -> p g q u", u=2)
+            if c_on_scalar(t):
+                nc.scalar.copy(out=dst, in_=src)
+            else:
+                nc.vector.tensor_copy(out=dst, in_=src)
+
+        def do_C(u):
             for j in range(UT):
-                t = u * UT + j
-                dst = gv[:, 2 * j : 2 * j + 2, 0:P, :]
-                src = xts[t][:].rearrange("p (g u) q -> p g q u", u=2)
-                if c_on_scalar(t):
-                    nc.scalar.copy(out=dst, in_=src)
-                else:
-                    nc.vector.tensor_copy(out=dst, in_=src)
+                c_tile(u * UT + j)
 
         def do_Z(u):
             codes = gpool.tile([P, UT * 2 * P], U32, name="codes", align_bytes=64)
@@ -247,12 +254,14 @@ def tile_modalityspecificposterior_t_kernel(tc, class_prototypes, query_features
                     accum_out=qts[:, t : t + 1],
                 )
 
-        def do_AB(u):
+        def do_A(u):
             for j in range(UT):
                 t = u * UT + j
                 nc.vector.scalar_tensor_tensor(
                     out=ds_t(t), in0=accs[t][:], scalar=2.0, in1=pt[:], op0=ALU.mult, op1=ALU.subtract,
                 )
+
+        def do_B(u):
             for j in range(UT):
                 t = u * UT + j
                 nc.vector.tensor_scalar(
@@ -267,25 +276,40 @@ def tile_modalityspecificposterior_t_kernel(tc, class_prototypes, query_features
                     out=ds_t(t), in_=ds_t(t), func=ACT.Sqrt, bias=q_of(t), scale=-1.0,
                 )
 
-        for s in range(-2, NU + 1):
-            if (s + 4) % 2 == 0 and 3 <= (s + 4) // 2 < NCH:
+        t_tile(0)
+        t_tile(1)
+        t_tile(2)
+        do_Q(0)
+        do_Q(1)
+        c_tile(0)
+        t_tile(3)
+        c_tile(1)
+        ptp = build_pt_rows()
+        c_tile(2)
+        c_tile(3)
+        do_Z(0)
+        do_M(0)
+        do_D(0)
+        nc.vector.tensor_copy(out=pt[:], in_=ptp[:])
+
+        for s in range(0, NU + 2):
+            if s % 2 == 0 and 3 <= (s + 4) // 2 < NCH:
                 load((s + 4) // 2)
-            if 0 <= s + 2 < NU:
+            if s + 2 < NU:
                 do_T(s + 2)
-            if 0 <= s + 1 < NU:
+            if s + 1 < NU:
                 do_Z(s + 1)
                 do_M(s + 1)
-                do_D(s + 1)
-            if 0 <= s + 2 < NU:
+            if s + 2 < NU:
                 do_C(s + 2)
-            if 0 <= s + 1 < NU:
-                do_Q(s + 1)
-            if s == -1:
-                build_pt()
-            if 0 <= s < NU:
-                do_AB(s)
-            if 0 <= s + 1 < NU:
-                do_X(s + 1)
+                do_Q(s + 2)
+            if s < NU:
+                do_A(s)
+                do_X(s)
+            if s + 1 < NU:
+                do_D(s + 1)
+            if s < NU:
+                do_B(s)
             if 0 <= s - 1 < NU:
                 do_R(s - 1)
 
@@ -325,6 +349,11 @@ def tile_modalityspecificposterior_t_kernel(tc, class_prototypes, query_features
                 else:
                     nc.vector.tensor_scalar_mul(out=ds_t(t), in0=es[t][:], scalar1=rs[:, t : t + 1])
 
+        stores = [(c * CT, c * CT + CT) for c in range(NCH - 1)] + [(NT - 4, NT - 2), (NT - 2, NT - 1), (NT - 1, NT)]
+
+        def n_step(t):
+            return t // UT + (1 if n_on_scalar(t) else 0)
+
         for s in range(-1, NU + 1):
             if 0 <= s + 1 < NU:
                 do_E(s + 1)
@@ -333,9 +362,9 @@ def tile_modalityspecificposterior_t_kernel(tc, class_prototypes, query_features
                 do_N(s, False)
             if 0 <= s - 1 < NU:
                 do_N(s - 1, True)
-                if (s - 1) % 2 == 1:
-                    c = (s - 1) // 2
-                    nc.sync.dma_start(out=ov[:, c * CT : (c + 1) * CT, :], in_=ds[c][:])
+            for a, b in stores:
+                if max(n_step(t) for t in range(a, b)) == s:
+                    nc.sync.dma_start(out=ov[:, a:b, :], in_=ds[a // CT][:, a % CT : a % CT + (b - a), :])
 
         nc.sync.dma_start(out=out_1.rearrange("(p t) -> p t", t=NT), in_=rs[:])
         nc.scalar.activation(out=lns[:], in_=ssum[:], func=ACT.Ln)

@@ -29,11 +29,11 @@ FLOPS = 2 * NQ * NK * D
 
 
 def c_on_scalar(t):
-    return t >= 4 and ((t // 2) % 4 != 3 or t % 2 == 0)
+    return t >= 4 and (diag(t | 1) or t % 2 == 0)
 
 
 def diag(t):
-    return t % 2 == 1 and (t // 2) % 4 != 3
+    return t % 2 == 1 and t >= 4 and (t // 2) % 6 != 1
 
 
 def n_on_scalar(t):

@@ -89,7 +89,7 @@ def tile_modalityspecificposterior_t_kernel(tc, class_prototypes, query_features
         hh = const.tile([P, NT], F32, name="hh")
         ps_sum = const.tile([P, 4], F32, name="ps_sum")
         ps_fix = const.tile([P, 4], F32, name="ps_fix")
-        junk = const.tile([P, D], BF16, name="junk")
+        junks = [const.tile([P, D], BF16, name="junk%d" % i) for i in range(2)]
         pt = const.tile([P, NK], F32, name="pt")
         rep = const.tile([P, 4, P], F32, name="rep")
 
@@ -129,7 +129,7 @@ def tile_modalityspecificposterior_t_kernel(tc, class_prototypes, query_features
                 in_=xt[:].rearrange("p (g u) r -> p g r u", u=2),
             )
             nc.scalar.activation(
-                out=junk[:], in_=p_sb[:, c, :], func=ACT.Square, bias=eps_neg[:], scale=1.0,
+                out=junks[c % 2][:], in_=p_sb[:, c, :], func=ACT.Square, bias=eps_neg[:], scale=1.0,
                 accum_out=ps_sum[:, c : c + 1],
             )
         gp_b = gp[:].bitcast(BF16)
@@ -250,7 +250,7 @@ def tile_modalityspecificposterior_t_kernel(tc, class_prototypes, query_features
                 if diag(t):
                     continue
                 nc.scalar.activation(
-                    out=junk[:], in_=qch[t // CT][:, t % CT, :], func=ACT.Square, bias=eps_pos[:], scale=1.0,
+                    out=junks[t % 2][:], in_=qch[t // CT][:, t % CT, :], func=ACT.Square, bias=eps_pos[:], scale=1.0,
                     accum_out=qts[:, t : t + 1],
                 )
 
@@ -331,13 +331,14 @@ def tile_modalityspecificposterior_t_kernel(tc, class_prototypes, query_features
 
         def do_H(u):
             t0 = u * UT
-            nc.vector.reciprocal(out=rs[:, t0 : t0 + UT], in_=ssum[:, t0 : t0 + UT])
             for j in range(UT):
                 t = t0 + j
                 nc.vector.scalar_tensor_tensor(
                     out=ds_t(t), in0=ds_t(t), scalar=dmin[:, t : t + 1], in1=es[t][:],
                     op0=ALU.subtract, op1=ALU.mult, accum_out=ed[:, t : t + 1],
                 )
+                if j == 0:
+                    nc.vector.reciprocal(out=rs[:, t0 : t0 + UT], in_=ssum[:, t0 : t0 + UT])
 
         def do_N(u, on_scalar):
             for j in range(UT):
@@ -349,7 +350,7 @@ def tile_modalityspecificposterior_t_kernel(tc, class_prototypes, query_features
                 else:
                     nc.vector.tensor_scalar_mul(out=ds_t(t), in0=es[t][:], scalar1=rs[:, t : t + 1])
 
-        stores = [(c * CT, c * CT + CT) for c in range(NCH - 1)] + [(NT - 4, NT - 2), (NT - 2, NT - 1), (NT - 1, NT)]
+        stores = [(u * UT, u * UT + UT) for u in range(NU - 1)] + [(NT - 2, NT - 1), (NT - 1, NT)]
 
         def n_step(t):
             return t // UT + (1 if n_on_scalar(t) else 0)

@@ -183,9 +183,10 @@ def tile_modalityspecificposterior_t_kernel(tc, class_prototypes, query_features
             else:
                 nc.vector.tensor_copy(out=dst, in_=src)
 
-        def do_C(u):
+        def do_C(u, on_scalar):
             for j in range(UT):
-                c_tile(u * UT + j)
+                if c_on_scalar(u * UT + j) == on_scalar:
+                    c_tile(u * UT + j)
 
         def do_Z(u):
             codes = gpool.tile([P, UT * 2 * P], U32, name="codes", align_bytes=64)
@@ -287,6 +288,7 @@ def tile_modalityspecificposterior_t_kernel(tc, class_prototypes, query_features
         ptp = build_pt_rows()
         c_tile(2)
         c_tile(3)
+        do_T(2)
         do_Z(0)
         do_M(0)
         do_D(0)
@@ -295,13 +297,13 @@ def tile_modalityspecificposterior_t_kernel(tc, class_prototypes, query_features
         for s in range(0, NU + 2):
             if s % 2 == 0 and 3 <= (s + 4) // 2 < NCH:
                 load((s + 4) // 2)
-            if s + 2 < NU:
+            if 0 < s and s + 2 < NU:
                 do_T(s + 2)
             if s + 1 < NU:
                 do_Z(s + 1)
                 do_M(s + 1)
             if s + 2 < NU:
-                do_C(s + 2)
+                do_C(s + 2, True)
                 do_Q(s + 2)
             if s < NU:
                 do_A(s)
@@ -310,6 +312,8 @@ def tile_modalityspecificposterior_t_kernel(tc, class_prototypes, query_features
                 do_D(s + 1)
             if s < NU:
                 do_B(s)
+            if s + 2 < NU:
+                do_C(s + 2, False)
             if 0 <= s - 1 < NU:
                 do_R(s - 1)
 

@@ -12,6 +12,8 @@ U8 = mybir.dt.uint8
 FP8X4 = mybir.dt.float8_e4m3fn_x4
 ACT = mybir.ActivationFunctionType
 ALU = mybir.AluOpType
+AX = mybir.AxisListType
+BIG = 3.0e38
 
 P = 128
 NQ, NK, D = 8192, 512, 1024
@@ -263,11 +265,17 @@ def tile_modalityspecificposterior_t_kernel(tc, class_prototypes, query_features
                 )
 
         def do_B(u):
+            t0 = u * UT
+            nc.vector.tensor_reduce(
+                out=um[:, t0 : t0 + UT], in_=ds[t0 // CT][:, t0 % CT : t0 % CT + UT, :], axis=AX.X, op=ALU.max,
+            )
+
+        def do_K(u):
             for j in range(UT):
                 t = u * UT + j
-                nc.vector.tensor_scalar(
-                    out=ds_t(t), in0=ds_t(t), scalar1=q_of(t), scalar2=None,
-                    op0=ALU.min, op1=ALU.max, accum_out=um[:, t : t + 1],
+                nc.gpsimd.tensor_scalar(
+                    out=ds_t(t), in0=ds_t(t), scalar1=q_of(t), scalar2=-BIG,
+                    op0=ALU.min, op1=ALU.max,
                 )
 
         def do_R(u):
@@ -294,7 +302,7 @@ def tile_modalityspecificposterior_t_kernel(tc, class_prototypes, query_features
         do_D(0)
         nc.vector.tensor_copy(out=pt[:], in_=ptp[:])
 
-        for s in range(0, NU + 2):
+        for s in range(0, NU + 3):
             if s % 2 == 0 and 3 <= (s + 4) // 2 < NCH:
                 load((s + 4) // 2)
             if 0 < s and s + 2 < NU:
@@ -308,14 +316,15 @@ def tile_modalityspecificposterior_t_kernel(tc, class_prototypes, query_features
             if s < NU:
                 do_A(s)
                 do_X(s)
+                do_K(s)
             if s + 1 < NU:
                 do_D(s + 1)
-            if s < NU:
-                do_B(s)
+            if 0 <= s - 1 < NU:
+                do_B(s - 1)
             if s + 2 < NU:
                 do_C(s + 2, False)
-            if 0 <= s - 1 < NU:
-                do_R(s - 1)
+            if 0 <= s - 2 < NU:
+                do_R(s - 2)
 
         nc.vector.tensor_add(out=qt[:], in0=qts[:], in1=qtv[:])
         nc.vector.tensor_sub(out=dm2[:], in0=qt[:], in1=um[:])

@@ -14,6 +14,7 @@ ACT = mybir.ActivationFunctionType
 ALU = mybir.AluOpType
 AX = mybir.AxisListType
 BIG = 3.0e38
+GTAIL = 2
 
 P = 128
 NQ, NK, D = 8192, 512, 1024
@@ -31,7 +32,7 @@ FLOPS = 2 * NQ * NK * D
 
 
 def c_on_scalar(t):
-    return t >= 4 and (diag(t | 1) or t % 2 == 0)
+    return t >= 4 and ((diag(t | 1) and (t // 2) % 6 != 4) or t % 2 == 0)
 
 
 def diag(t):
@@ -264,11 +265,22 @@ def tile_modalityspecificposterior_t_kernel(tc, class_prototypes, query_features
                     out=ds_t(t), in0=accs[t][:], scalar=2.0, in1=pt[:], op0=ALU.mult, op1=ALU.subtract,
                 )
 
+        def on_gpsimd(u):
+            return u < NU - GTAIL
+
         def do_B(u):
             t0 = u * UT
-            nc.vector.tensor_reduce(
-                out=um[:, t0 : t0 + UT], in_=ds[t0 // CT][:, t0 % CT : t0 % CT + UT, :], axis=AX.X, op=ALU.max,
-            )
+            if on_gpsimd(u):
+                nc.vector.tensor_reduce(
+                    out=um[:, t0 : t0 + UT], in_=ds[t0 // CT][:, t0 % CT : t0 % CT + UT, :], axis=AX.X, op=ALU.max,
+                )
+                return
+            for j in range(UT):
+                t = t0 + j
+                nc.vector.tensor_scalar(
+                    out=ds_t(t), in0=ds_t(t), scalar1=q_of(t), scalar2=None,
+                    op0=ALU.min, op1=ALU.max, accum_out=um[:, t : t + 1],
+                )
 
         def do_K(u):
             for j in range(UT):
@@ -302,7 +314,7 @@ def tile_modalityspecificposterior_t_kernel(tc, class_prototypes, query_features
         do_D(0)
         nc.vector.tensor_copy(out=pt[:], in_=ptp[:])
 
-        for s in range(0, NU + 3):
+        for s in range(0, NU + 2):
             if s % 2 == 0 and 3 <= (s + 4) // 2 < NCH:
                 load((s + 4) // 2)
             if 0 < s and s + 2 < NU:
@@ -316,15 +328,20 @@ def tile_modalityspecificposterior_t_kernel(tc, class_prototypes, query_features
             if s < NU:
                 do_A(s)
                 do_X(s)
-                do_K(s)
+                if on_gpsimd(s):
+                    do_K(s)
             if s + 1 < NU:
                 do_D(s + 1)
-            if 0 <= s - 1 < NU:
+            if 0 <= s - 1 < NU and on_gpsimd(s - 1):
                 do_B(s - 1)
+            if s < NU and not on_gpsimd(s):
+                do_B(s)
             if s + 2 < NU:
                 do_C(s + 2, False)
-            if 0 <= s - 2 < NU:
+            if 0 <= s - 2 < NU and on_gpsimd(s - 2):
                 do_R(s - 2)
+            if 0 <= s - 1 < NU and not on_gpsimd(s - 1):
+                do_R(s - 1)
 
         nc.vector.tensor_add(out=qt[:], in0=qts[:], in1=qtv[:])
         nc.vector.tensor_sub(out=dm2[:], in0=qt[:], in1=um[:])

@@ -14,7 +14,7 @@ ACT = mybir.ActivationFunctionType
 ALU = mybir.AluOpType
 AX = mybir.AxisListType
 BIG = 3.0e38
-GTAIL = 2
+TAIL = 3
 
 P = 128
 NQ, NK, D = 8192, 512, 1024
@@ -266,21 +266,29 @@ def tile_modalityspecificposterior_t_kernel(tc, class_prototypes, query_features
                 )
 
         def on_gpsimd(u):
-            return u < NU - GTAIL
+            return not late(u)
+
+        def late(u):
+            return u >= NU - TAIL
 
         def do_B(u):
             t0 = u * UT
-            if on_gpsimd(u):
-                nc.vector.tensor_reduce(
-                    out=um[:, t0 : t0 + UT], in_=ds[t0 // CT][:, t0 % CT : t0 % CT + UT, :], axis=AX.X, op=ALU.max,
-                )
-                return
+            nc.vector.tensor_reduce(
+                out=um[:, t0 : t0 + UT], in_=ds[t0 // CT][:, t0 % CT : t0 % CT + UT, :], axis=AX.X, op=ALU.max,
+            )
+
+        def do_KV(u):
             for j in range(UT):
-                t = t0 + j
+                t = u * UT + j
                 nc.vector.tensor_scalar(
-                    out=ds_t(t), in0=ds_t(t), scalar1=q_of(t), scalar2=None,
-                    op0=ALU.min, op1=ALU.max, accum_out=um[:, t : t + 1],
+                    out=ds_t(t), in0=ds_t(t), scalar1=q_of(t), scalar2=-BIG, op0=ALU.min, op1=ALU.max,
                 )
+
+        def do_Bmin(u):
+            t0 = u * UT
+            nc.vector.tensor_reduce(
+                out=dmin[:, t0 : t0 + UT], in_=ds[t0 // CT][:, t0 % CT : t0 % CT + UT, :], axis=AX.X, op=ALU.min,
+            )
 
         def do_K(u):
             for j in range(UT):
@@ -317,25 +325,28 @@ def tile_modalityspecificposterior_t_kernel(tc, class_prototypes, query_features
         for s in range(0, NU + 2):
             if s % 2 == 0 and 3 <= (s + 4) // 2 < NCH:
                 load((s + 4) // 2)
-            if 0 < s and s + 2 < NU:
-                do_T(s + 2)
             if s + 1 < NU:
                 do_Z(s + 1)
+            if s + 1 < NU:
                 do_M(s + 1)
             if s + 2 < NU:
                 do_C(s + 2, True)
+            if s + 3 < NU:
+                do_T(s + 3)
+            if s + 2 < NU:
                 do_Q(s + 2)
             if s < NU:
                 do_A(s)
+            if s < NU:
                 do_X(s)
-                if on_gpsimd(s):
-                    do_K(s)
+            if s < NU and on_gpsimd(s):
+                do_K(s)
+            if s < NU and not on_gpsimd(s):
+                do_KV(s)
             if s + 1 < NU:
                 do_D(s + 1)
-            if 0 <= s - 1 < NU and on_gpsimd(s - 1):
+            if 0 <= s - 1 < NU and not late(s - 1):
                 do_B(s - 1)
-            if s < NU and not on_gpsimd(s):
-                do_B(s)
             if s + 2 < NU:
                 do_C(s + 2, False)
             if 0 <= s - 2 < NU and on_gpsimd(s - 2):
@@ -343,9 +354,14 @@ def tile_modalityspecificposterior_t_kernel(tc, class_prototypes, query_features
             if 0 <= s - 1 < NU and not on_gpsimd(s - 1):
                 do_R(s - 1)
 
-        nc.vector.tensor_add(out=qt[:], in0=qts[:], in1=qtv[:])
-        nc.vector.tensor_sub(out=dm2[:], in0=qt[:], in1=um[:])
-        nc.scalar.activation(out=dmin[:], in_=dm2[:], func=ACT.Sqrt)
+            if s == NU - TAIL + 1:
+                n = (NU - TAIL) * UT
+                nc.vector.tensor_add(out=qt[:, 0:n], in0=qts[:, 0:n], in1=qtv[:, 0:n])
+                nc.vector.tensor_sub(out=dm2[:, 0:n], in0=qt[:, 0:n], in1=um[:, 0:n])
+                nc.scalar.activation(out=dmin[:, 0:n], in_=dm2[:, 0:n], func=ACT.Sqrt)
+
+        for u in range(NU - TAIL, NU):
+            do_Bmin(u)
 
         es = {}
 

@@ -15,6 +15,7 @@ ALU = mybir.AluOpType
 AX = mybir.AxisListType
 BIG = 3.0e38
 TAIL = 3
+HALF = 16
 
 P = 128
 NQ, NK, D = 8192, 512, 1024
@@ -32,7 +33,7 @@ FLOPS = 2 * NQ * NK * D
 
 
 def c_on_scalar(t):
-    return t >= 4 and ((diag(t | 1) and (t // 2) % 6 != 4) or t % 2 == 0)
+    return (t >= 4 and ((diag(t | 1) and (t // 2) % 6 != 4) or t % 2 == 0)) or (t >= 2 * HALF and t % 4 != 1)
 
 
 def diag(t):
@@ -101,10 +102,17 @@ def tile_modalityspecificposterior_t_kernel(tc, class_prototypes, query_features
         p_codes = const.tile([P, 2, NK], U32, name="p_codes", align_bytes=64)
         p_scales = const.tile([P, 2, NK], U8, name="p_scales", align_bytes=64)
 
-        ds = [keep.tile([P, CT, NK], F32, name="ds%d" % c) for c in range(NCH)]
+        RT = max(HALF, NU - HALF) * UT
+        ds = [keep.tile([P, CT, NK], F32, name="ds%d" % c) for c in range((RT + CT - 1) // CT)]
+        e1 = [keep.tile([P, UT, NK], F32, name="e%d" % u) for u in range(HALF)]
 
         def ds_t(t):
-            return ds[t // CT][:, t % CT, :]
+            r = t if t < HALF * UT else t - HALF * UT
+            return ds[r // CT][:, r % CT, :]
+
+        def ds_u(u):
+            r = (u if u < HALF else u - HALF) * UT
+            return ds[r // CT][:, r % CT : r % CT + UT, :]
 
         for c in range(4):
             nc.sync.dma_start(out=p_sb[:, c, :], in_=pv[:, c, :])
@@ -121,26 +129,32 @@ def tile_modalityspecificposterior_t_kernel(tc, class_prototypes, query_features
         load(1)
         load(2)
 
-        gp_v = gp[:].rearrange("p (g k u) -> p g k u", g=2, u=2)
+        gp_v = gp[:].rearrange("p (c g k u) -> p c g k u", c=4, g=2, u=2)
+        gp_b = gp[:].bitcast(BF16)
+
+        def quantise_p(c):
+            for g in range(2):
+                o = (c * 2 + g) * 4 * P
+                nc.vector.quantize_mx(
+                    out=p_codes[:, g, c * P : (c + 1) * P].bitcast(FP8X4),
+                    scales=p_scales[:, g, c * P : (c + 1) * P],
+                    in_=gp_b[:, o : o + 4 * P],
+                )
+
         p_w = p_sb[:].bitcast(F32)
         for c in range(4):
             xt = ps_t.tile([P, 4, P], F32, name="xt")
             for b in range(4):
                 nc.tensor.transpose(xt[:, b, :], p_w[:, c, b * P : (b + 1) * P], ident)
             nc.vector.tensor_copy(
-                out=gp_v[:, :, c * P : (c + 1) * P, :],
+                out=gp_v[:, c, :, :, :],
                 in_=xt[:].rearrange("p (g u) r -> p g r u", u=2),
             )
+            if c > 0:
+                quantise_p(c - 1)
             nc.scalar.activation(
                 out=junks[c % 2][:], in_=p_sb[:, c, :], func=ACT.Square, bias=eps_neg[:], scale=1.0,
                 accum_out=ps_sum[:, c : c + 1],
-            )
-        gp_b = gp[:].bitcast(BF16)
-        for g in range(2):
-            nc.vector.quantize_mx(
-                out=p_codes[:, g, :].bitcast(FP8X4),
-                scales=p_scales[:, g, :],
-                in_=gp_b[:, g * 4 * NK : (g + 1) * 4 * NK],
             )
 
         def build_pt_rows():
@@ -265,16 +279,13 @@ def tile_modalityspecificposterior_t_kernel(tc, class_prototypes, query_features
                     out=ds_t(t), in0=accs[t][:], scalar=2.0, in1=pt[:], op0=ALU.mult, op1=ALU.subtract,
                 )
 
-        def on_gpsimd(u):
-            return not late(u)
-
         def late(u):
-            return u >= NU - TAIL
+            return HALF - TAIL <= u < HALF or u >= NU - TAIL
 
         def do_B(u):
             t0 = u * UT
             nc.vector.tensor_reduce(
-                out=um[:, t0 : t0 + UT], in_=ds[t0 // CT][:, t0 % CT : t0 % CT + UT, :], axis=AX.X, op=ALU.max,
+                out=um[:, t0 : t0 + UT], in_=ds_u(u), axis=AX.X, op=ALU.max,
             )
 
         def do_KV(u):
@@ -284,10 +295,18 @@ def tile_modalityspecificposterior_t_kernel(tc, class_prototypes, query_features
                     out=ds_t(t), in0=ds_t(t), scalar1=q_of(t), scalar2=-BIG, op0=ALU.min, op1=ALU.max,
                 )
 
+        def do_BV(u):
+            for j in range(UT):
+                t = u * UT + j
+                nc.vector.tensor_scalar(
+                    out=ds_t(t), in0=ds_t(t), scalar1=q_of(t), scalar2=None,
+                    op0=ALU.min, op1=ALU.max, accum_out=um[:, t : t + 1],
+                )
+
         def do_Bmin(u):
             t0 = u * UT
             nc.vector.tensor_reduce(
-                out=dmin[:, t0 : t0 + UT], in_=ds[t0 // CT][:, t0 % CT : t0 % CT + UT, :], axis=AX.X, op=ALU.min,
+                out=dmin[:, t0 : t0 + UT], in_=ds_u(u), axis=AX.X, op=ALU.min,
             )
 
         def do_K(u):
@@ -305,12 +324,78 @@ def tile_modalityspecificposterior_t_kernel(tc, class_prototypes, query_features
                     out=ds_t(t), in_=ds_t(t), func=ACT.Sqrt, bias=q_of(t), scale=-1.0,
                 )
 
+        es = {}
+
+        def new_e():
+            e = epool.tile([P, NK], F32, name="e")
+            return e[:]
+
+        def do_E(u):
+            for j in range(UT):
+                t = u * UT + j
+                e = e1[u][:, j, :] if u < HALF else new_e()
+                nc.scalar.activation(
+                    out=e, in_=ds_t(t), func=ACT.Exp, bias=dmin[:, t : t + 1], scale=-1.0,
+                    accum_out=ssum[:, t : t + 1],
+                )
+                es[t] = e
+
+        def do_H(u):
+            t0 = u * UT
+            for j in range(UT):
+                t = t0 + j
+                nc.vector.scalar_tensor_tensor(
+                    out=ds_t(t), in0=ds_t(t), scalar=dmin[:, t : t + 1], in1=es[t],
+                    op0=ALU.subtract, op1=ALU.mult, accum_out=ed[:, t : t + 1],
+                )
+                if j == 0 and u >= HALF:
+                    do_S(u)
+
+        def do_S(u):
+            t0 = u * UT
+            nc.vector.reciprocal(out=rs[:, t0 : t0 + UT], in_=ssum[:, t0 : t0 + UT])
+
+        def do_N(u, on_scalar):
+            for j in range(UT):
+                t = u * UT + j
+                if n_on_scalar(t) != on_scalar:
+                    continue
+                if on_scalar:
+                    nc.scalar.activation(out=ds_t(t), in_=es[t], func=ACT.Copy, scale=rs[:, t : t + 1])
+                else:
+                    nc.vector.tensor_scalar_mul(out=ds_t(t), in0=es[t], scalar1=rs[:, t : t + 1])
+
+        def do_NG(u):
+            for j in range(UT):
+                t = u * UT + j
+                nc.gpsimd.tensor_scalar(
+                    out=es[t], in0=es[t], scalar1=rs[:, t : t + 1], scalar2=1.0, op0=ALU.mult, op1=ALU.mult,
+                )
+
+        def do_dmin(lo, hi):
+            a, b = lo * UT, (hi - TAIL) * UT
+            nc.vector.tensor_add(out=qt[:, a:b], in0=qts[:, a:b], in1=qtv[:, a:b])
+            nc.vector.tensor_sub(out=dm2[:, a:b], in0=qt[:, a:b], in1=um[:, a:b])
+            nc.scalar.activation(out=dmin[:, a:b], in_=dm2[:, a:b], func=ACT.Sqrt)
+
+        stores = [(u * UT, u * UT + UT) for u in range(HALF, NU - 1)] + [(NT - 2, NT - 1), (NT - 1, NT)]
+
+        def n_step(t):
+            return t // UT + (1 if n_on_scalar(t) else 0)
+
+        def deferred(i):
+            n = NU - HALF - TAIL
+            if i >= n:
+                return []
+            return list(range(i * HALF // n, (i + 1) * HALF // n))
+
         t_tile(0)
         t_tile(1)
         t_tile(2)
         do_Q(0)
         do_Q(1)
         c_tile(0)
+        quantise_p(3)
         t_tile(3)
         c_tile(1)
         ptp = build_pt_rows()
@@ -322,96 +407,68 @@ def tile_modalityspecificposterior_t_kernel(tc, class_prototypes, query_features
         do_D(0)
         nc.vector.tensor_copy(out=pt[:], in_=ptp[:])
 
-        for s in range(0, NU + 2):
-            if s % 2 == 0 and 3 <= (s + 4) // 2 < NCH:
-                load((s + 4) // 2)
-            if s + 1 < NU:
-                do_Z(s + 1)
-            if s + 1 < NU:
-                do_M(s + 1)
-            if s + 2 < NU:
-                do_C(s + 2, True)
-            if s + 3 < NU:
-                do_T(s + 3)
-            if s + 2 < NU:
-                do_Q(s + 2)
-            if s < NU:
-                do_A(s)
-            if s < NU:
-                do_X(s)
-            if s < NU and on_gpsimd(s):
-                do_K(s)
-            if s < NU and not on_gpsimd(s):
-                do_KV(s)
-            if s + 1 < NU:
-                do_D(s + 1)
-            if 0 <= s - 1 < NU and not late(s - 1):
-                do_B(s - 1)
-            if s + 2 < NU:
-                do_C(s + 2, False)
-            if 0 <= s - 2 < NU and on_gpsimd(s - 2):
-                do_R(s - 2)
-            if 0 <= s - 1 < NU and not on_gpsimd(s - 1):
-                do_R(s - 1)
-
-            if s == NU - TAIL + 1:
-                n = (NU - TAIL) * UT
-                nc.vector.tensor_add(out=qt[:, 0:n], in0=qts[:, 0:n], in1=qtv[:, 0:n])
-                nc.vector.tensor_sub(out=dm2[:, 0:n], in0=qt[:, 0:n], in1=um[:, 0:n])
-                nc.scalar.activation(out=dmin[:, 0:n], in_=dm2[:, 0:n], func=ACT.Sqrt)
-
-        for u in range(NU - TAIL, NU):
-            do_Bmin(u)
-
-        es = {}
-
-        def do_E(u):
-            for j in range(UT):
-                t = u * UT + j
-                e = epool.tile([P, NK], F32, name="e")
-                nc.scalar.activation(
-                    out=e[:], in_=ds_t(t), func=ACT.Exp, bias=dmin[:, t : t + 1], scale=-1.0,
-                    accum_out=ssum[:, t : t + 1],
-                )
-                es[t] = e
-
-        def do_H(u):
-            t0 = u * UT
-            for j in range(UT):
-                t = t0 + j
-                nc.vector.scalar_tensor_tensor(
-                    out=ds_t(t), in0=ds_t(t), scalar=dmin[:, t : t + 1], in1=es[t][:],
-                    op0=ALU.subtract, op1=ALU.mult, accum_out=ed[:, t : t + 1],
-                )
-                if j == 0:
-                    nc.vector.reciprocal(out=rs[:, t0 : t0 + UT], in_=ssum[:, t0 : t0 + UT])
-
-        def do_N(u, on_scalar):
-            for j in range(UT):
-                t = u * UT + j
-                if n_on_scalar(t) != on_scalar:
-                    continue
-                if on_scalar:
-                    nc.scalar.activation(out=ds_t(t), in_=es[t][:], func=ACT.Copy, scale=rs[:, t : t + 1])
-                else:
-                    nc.vector.tensor_scalar_mul(out=ds_t(t), in0=es[t][:], scalar1=rs[:, t : t + 1])
-
-        stores = [(u * UT, u * UT + UT) for u in range(NU - 1)] + [(NT - 2, NT - 1), (NT - 1, NT)]
-
-        def n_step(t):
-            return t // UT + (1 if n_on_scalar(t) else 0)
-
-        for s in range(-1, NU + 1):
-            if 0 <= s + 1 < NU:
-                do_E(s + 1)
-            if 0 <= s < NU:
-                do_H(s)
-                do_N(s, False)
-            if 0 <= s - 1 < NU:
-                do_N(s - 1, True)
-            for a, b in stores:
-                if max(n_step(t) for t in range(a, b)) == s:
-                    nc.sync.dma_start(out=ov[:, a:b, :], in_=ds[a // CT][:, a % CT : a % CT + (b - a), :])
+        for lo, hi in ((0, HALF), (HALF, NU)):
+            first = lo == 0
+            for s in range(lo, hi + 1):
+                if s % 2 == 0 and 3 <= (s + 4) // 2 < NCH and s < hi:
+                    load((s + 4) // 2)
+                inner = s < hi
+                if inner and s + 1 < NU:
+                    do_Z(s + 1)
+                    do_M(s + 1)
+                for r in deferred(s - lo) if inner and not first else []:
+                    do_S(r)
+                    do_NG(r)
+                if inner and s + 2 < NU and not (first and s == hi - 1):
+                    do_C(s + 2, True)
+                    if s + 3 < NU:
+                        do_T(s + 3)
+                    do_Q(s + 2)
+                if inner:
+                    do_A(s)
+                    do_X(s)
+                    if late(s):
+                        do_KV(s)
+                    elif first:
+                        do_K(s)
+                    else:
+                        do_BV(s)
+                if inner and s + 1 < NU:
+                    do_D(s + 1)
+                if first and s - 1 >= lo and not late(s - 1):
+                    do_B(s - 1)
+                if inner and s + 2 < NU and not (first and s == hi - 1):
+                    do_C(s + 2, False)
+                if first and s - 2 >= lo and not late(s - 2):
+                    do_R(s - 2)
+                if s - 1 >= lo and (late(s - 1) or not first):
+                    do_R(s - 1)
+                if s == hi - TAIL + 1:
+                    do_dmin(lo, hi)
+                for r in deferred(s - lo) if inner and not first else []:
+                    nc.sync.dma_start(out=ov[:, r * UT : r * UT + UT, :], in_=e1[r][:])
+            for u in range(hi - TAIL, hi):
+                do_Bmin(u)
+            for s in range(lo - 1, hi + 1):
+                if lo <= s + 1 < hi:
+                    do_E(s + 1)
+                    if first and s + 1 == hi - 1:
+                        do_C(hi + 1, True)
+                        do_T(hi + 2)
+                        do_Q(hi + 1)
+                if lo <= s < hi:
+                    do_H(s)
+                    if not first:
+                        do_N(s, False)
+                if lo <= s - 1 < hi and not first:
+                    do_N(s - 1, True)
+                if first and s == hi:
+                    do_C(hi + 1, False)
+                if not first:
+                    for a, b in stores:
+                        if max(n_step(t) for t in range(a, b)) == s:
+                            r = a - HALF * UT
+                            nc.sync.dma_start(out=ov[:, a:b, :], in_=ds[r // CT][:, r % CT : r % CT + (b - a), :])
 
         nc.sync.dma_start(out=out_1.rearrange("(p t) -> p t", t=NT), in_=rs[:])
         nc.scalar.activation(out=lns[:], in_=ssum[:], func=ACT.Ln)

from contextlib import ExitStack

import concourse.bass as bass
import concourse.mybir as mybir
import concourse.tile as tile
from concourse.masks import make_identity

F32 = mybir.dt.float32
BF16 = mybir.dt.bfloat16
U32 = mybir.dt.uint32
U8 = mybir.dt.uint8
FP8X4 = mybir.dt.float8_e4m3fn_x4
ACT = mybir.ActivationFunctionType
ALU = mybir.AluOpType
AX = mybir.AxisListType
BIG = 3.0e38
TAIL = 3
HALF = 16

P = 128
NQ, NK, D = 8192, 512, 1024
EPS = 1e-6
NT = NQ // P
UT = 2
NU = NT // UT
CT = 4
NCH = NT // CT
W = D // 2
QS = 136
NB = UT * 2
C0 = D * EPS * EPS / (1.0 + 2.0 * EPS)
FLOPS = 2 * NQ * NK * D


def c_on_scalar(t):
    return (t >= 4 and ((diag(t | 1) and (t // 2) % 6 != 4) or t % 2 == 0)) or (t >= 2 * HALF and t % 4 != 1)


def diag(t):
    return t % 2 == 1 and t >= 4 and (t // 2) % 6 != 1


def n_on_scalar(t):
    return t % 8 in (1, 3, 5) and t < 60


def tile_modalityspecificposterior_t_kernel(tc, class_prototypes, query_features, out_0, out_1, out_2):
    nc = tc.nc
    qv = query_features.rearrange("(p t) d -> p t d", t=NT)
    ov = out_0.rearrange("(p t) k -> p t k", t=NT)
    pv = class_prototypes.rearrange("(c r) d -> r c d", r=P)

    with ExitStack() as ctx:
        ctx.enter_context(tc.manual_schedule())
        const = ctx.enter_context(tc.tile_pool(name="const", bufs=1))
        keep = ctx.enter_context(tc.tile_pool(name="keep", bufs=1))
        qpool = ctx.enter_context(tc.tile_pool(name="qpool", bufs=3))
        gpool = ctx.enter_context(tc.tile_pool(name="gpool", bufs=3))
        gfix = ctx.enter_context(tc.tile_pool(name="gfix", bufs=1))
        epool = ctx.enter_context(tc.tile_pool(name="epool", bufs=8))
        ps_t = ctx.enter_context(tc.psum_pool(name="ps_t", bufs=3))
        ps_d = ctx.enter_context(tc.psum_pool(name="ps_d", bufs=1))
        ps_a = ctx.enter_context(tc.psum_pool(name="ps_a", bufs=4))

        mask = const.tile([P, P + 4], F32, name="mask")
        ident = mask[:, 0:P]
        make_identity(nc, ident)
        nc.vector.memset(mask[:, P : P + 1], 2.0 * EPS)
        junkd = const.tile([P, P + 4], F32, name="junkd")
        gbuf = [gfix.tile([P, NB * QS * 2], F32, name="grp%d" % i, align_bytes=64) for i in range(3)]
        for i in range(3):
            ones = gbuf[i][:].bitcast(BF16).rearrange("p (b s t) -> p b s t", b=NB, t=4)
            nc.vector.memset(ones[:, :, P, :], 1.0)
        eps_pos = const.tile([P, 1], F32, name="eps_pos")
        eps_neg = const.tile([P, 1], F32, name="eps_neg")
        warm = const.tile([P, 1], F32, name="warm")
        nc.vector.memset(eps_pos[:], EPS)
        nc.vector.memset(eps_neg[:], -EPS)
        nc.scalar.activation(out=warm[:], in_=eps_pos[:], func=ACT.Sqrt)

        qt = const.tile([P, NT], F32, name="qt")
        qts = const.tile([P, NT], F32, name="qts")
        qtv = const.tile([P, NT], F32, name="qtv")
        nc.vector.memset(qts[:], 0.0)
        nc.vector.memset(qtv[:], 0.0)
        um = const.tile([P, NT], F32, name="um")
        dm2 = const.tile([P, NT], F32, name="dm2")
        dmin = const.tile([P, NT], F32, name="dmin")
        ssum = const.tile([P, NT], F32, name="ssum")
        rs = const.tile([P, NT], F32, name="rs")
        ed = const.tile([P, NT], F32, name="ed")
        lns = const.tile([P, NT], F32, name="lns")
        hh = const.tile([P, NT], F32, name="hh")
        ps_sum = const.tile([P, 4], F32, name="ps_sum")
        ps_fix = const.tile([P, 4], F32, name="ps_fix")
        junks = [const.tile([P, D], BF16, name="junk%d" % i) for i in range(2)]
        pt = const.tile([P, NK], F32, name="pt")
        rep = const.tile([P, 4, P], F32, name="rep")

        p_sb = const.tile([P, 4, D], BF16, name="p_sb")
        gp = const.tile([P, 2 * NK * 2], F32, name="gp", align_bytes=64)
        p_codes = const.tile([P, 2, NK], U32, name="p_codes", align_bytes=64)
        p_scales = const.tile([P, 2, NK], U8, name="p_scales", align_bytes=64)

        RT = max(HALF, NU - HALF) * UT
        ds = [keep.tile([P, CT, NK], F32, name="ds%d" % c) for c in range((RT + CT - 1) // CT)]
        e1 = [keep.tile([P, UT, NK], F32, name="e%d" % u) for u in range(HALF)]

        def ds_t(t):
            r = t if t < HALF * UT else t - HALF * UT
            return ds[r // CT][:, r % CT, :]

        def ds_u(u):
            r = (u if u < HALF else u - HALF) * UT
            return ds[r // CT][:, r % CT : r % CT + UT, :]

        for c in range(4):
            nc.sync.dma_start(out=p_sb[:, c, :], in_=pv[:, c, :])
        qch = {}

        def load(c, pieces=1):
            qc = qpool.tile([P, CT, D], BF16, name="qc")
            n = CT // pieces
            for i in range(pieces):
                nc.sync.dma_start(out=qc[:, i * n : (i + 1) * n, :], in_=qv[:, c * CT + i * n : c * CT + (i + 1) * n, :])
            qch[c] = qc

        load(0, 2)
        load(1)
        load(2)

        gp_v = gp[:].rearrange("p (c g k u) -> p c g k u", c=4, g=2, u=2)
        gp_b = gp[:].bitcast(BF16)

        def quantise_p(c):
            for g in range(2):
                o = (c * 2 + g) * 4 * P
                nc.vector.quantize_mx(
                    out=p_codes[:, g, c * P : (c + 1) * P].bitcast(FP8X4),
                    scales=p_scales[:, g, c * P : (c + 1) * P],
                    in_=gp_b[:, o : o + 4 * P],
                )

        p_w = p_sb[:].bitcast(F32)
        for c in range(4):
            xt = ps_t.tile([P, 4, P], F32, name="xt")
            for b in range(4):
                nc.tensor.transpose(xt[:, b, :], p_w[:, c, b * P : (b + 1) * P], ident)
            nc.vector.tensor_copy(
                out=gp_v[:, c, :, :, :],
                in_=xt[:].rearrange("p (g u) r -> p g r u", u=2),
            )
            if c > 0:
                quantise_p(c - 1)
            nc.scalar.activation(
                out=junks[c % 2][:], in_=p_sb[:, c, :], func=ACT.Square, bias=eps_neg[:], scale=1.0,
                accum_out=ps_sum[:, c : c + 1],
            )

        def build_pt_rows():
            nc.vector.tensor_scalar_add(out=ps_fix[:], in0=ps_sum[:], scalar1=-(D * EPS * EPS))
            for c in range(4):
                nc.vector.tensor_scalar(
                    out=rep[:, c, :], in0=ident, scalar1=0.0, scalar2=ps_fix[:, c : c + 1],
                    op0=ALU.mult, op1=ALU.add,
                )
            ptp = ps_a.tile([P, NK], F32, name="acc")
            for c in range(4):
                nc.tensor.transpose(ptp[:, c * P : (c + 1) * P], rep[:, c, :], ident)
            return ptp

        xts = {}
        grp = {}
        cod = {}
        accs = {}

        def t_tile(t):
            qw = qch[t // CT][:].bitcast(F32)
            xt = ps_t.tile([P, 4, P], F32, name="xt")
            for b in range(4):
                nc.tensor.transpose(xt[:, b, :], qw[:, t % CT, b * P : (b + 1) * P], ident)
            xts[t] = xt

        def do_T(u):
            for j in range(UT):
                t_tile(u * UT + j)

        def q_of(t):
            return qtv[:, t : t + 1] if diag(t) else qts[:, t : t + 1]

        def c_tile(t):
            u, j = t // UT, t % UT
            g = gbuf[u % 3]
            grp[u] = g
            gv = g[:].rearrange("p (b s u) -> p b s u", b=NB, u=2)
            dst = gv[:, 2 * j : 2 * j + 2, 0:P, :]
            src = xts[t][:].rearrange("p (g u) q -> p g q u", u=2)
            if c_on_scalar(t):
                nc.scalar.copy(out=dst, in_=src)
            else:
                nc.vector.tensor_copy(out=dst, in_=src)

        def do_C(u, on_scalar):
            for j in range(UT):
                if c_on_scalar(u * UT + j) == on_scalar:
                    c_tile(u * UT + j)

        def do_Z(u):
            codes = gpool.tile([P, UT * 2 * P], U32, name="codes", align_bytes=64)
            scales = gpool.tile([P, UT * 2 * P], U8, name="scales", align_bytes=64)
            gb = grp[u][:].bitcast(BF16)
            for b in range(NB):
                nc.vector.quantize_mx(
                    out=codes[:, b * P : (b + 1) * P].bitcast(FP8X4),
                    scales=scales[:, b * P : (b + 1) * P],
                    in_=gb[:, b * QS * 4 : b * QS * 4 + 4 * P],
                )
            cod[u] = (codes, scales)

        gds = {}

        def do_D(u):
            gb = grp[u][:].bitcast(BF16).rearrange("p (b s t) -> p b s t", b=NB, t=4)
            for j in range(UT):
                t = u * UT + j
                if not diag(t):
                    continue
                gd = ps_d.tile([P, NK], F32, name="gd")
                for i in range(8):
                    b, v = 2 * j + i // 4, i % 4
                    nc.tensor.matmul(
                        out=gd[:, 0 : P + 1], lhsT=gb[:, b, 0:P, v], rhs=gb[:, b, 0 : P + 1, v],
                        start=(i == 0), stop=(i == 7),
                    )
                gds[t] = gd

        def do_X(u):
            for j in range(UT):
                t = u * UT + j
                if not diag(t):
                    continue
                nc.vector.scalar_tensor_tensor(
                    out=junkd[:, 0 : P + 1], in0=gds[t][:, 0 : P + 1], scalar=C0, in1=mask[:, 0 : P + 1],
                    op0=ALU.add, op1=ALU.mult, accum_out=qtv[:, t : t + 1],
                )

        def do_M(u):
            codes, scales = cod[u]
            for j in range(UT):
                t = u * UT + j
                acc = ps_a.tile([P, NK], F32, name="acc")
                for g in range(2):
                    o = (j * 2 + g) * P
                    nc.tensor.matmul_mx(
                        out=acc[:],
                        lhsT=codes[:, o : o + P].bitcast(FP8X4),
                        lhsT_scale=scales[:, o : o + P],
                        rhs=p_codes[:, g, :].bitcast(FP8X4),
                        rhs_scale=p_scales[:, g, :],
                        start=(g == 0),
                        stop=(g == 1),
                    )
                accs[t] = acc

        def do_Q(u):
            for j in range(UT):
                t = u * UT + j
                if diag(t):
                    continue
                nc.scalar.activation(
                    out=junks[t % 2][:], in_=qch[t // CT][:, t % CT, :], func=ACT.Square, bias=eps_pos[:], scale=1.0,
                    accum_out=qts[:, t : t + 1],
                )

        def do_A(u):
            for j in range(UT):
                t = u * UT + j
                nc.vector.scalar_tensor_tensor(
                    out=ds_t(t), in0=accs[t][:], scalar=2.0, in1=pt[:], op0=ALU.mult, op1=ALU.subtract,
                )

        def late(u):
            return HALF - TAIL <= u < HALF or u >= NU - TAIL

        def do_B(u):
            t0 = u * UT
            nc.vector.tensor_reduce(
                out=um[:, t0 : t0 + UT], in_=ds_u(u), axis=AX.X, op=ALU.max,
            )

        def do_KV(u):
            for j in range(UT):
                t = u * UT + j
                nc.vector.tensor_scalar(
                    out=ds_t(t), in0=ds_t(t), scalar1=q_of(t), scalar2=-BIG, op0=ALU.min, op1=ALU.max,
                )

        def do_BV(u):
            for j in range(UT):
                t = u * UT + j
                nc.vector.tensor_scalar(
                    out=ds_t(t), in0=ds_t(t), scalar1=q_of(t), scalar2=None,
                    op0=ALU.min, op1=ALU.max, accum_out=um[:, t : t + 1],
                )

        def do_Bmin(u):
            t0 = u * UT
            nc.vector.tensor_reduce(
                out=dmin[:, t0 : t0 + UT], in_=ds_u(u), axis=AX.X, op=ALU.min,
            )

        def do_K(u):
            for j in range(UT):
                t = u * UT + j
                nc.gpsimd.tensor_scalar(
                    out=ds_t(t), in0=ds_t(t), scalar1=q_of(t), scalar2=-BIG,
                    op0=ALU.min, op1=ALU.max,
                )

        def do_R(u):
            for j in range(UT):
                t = u * UT + j
                nc.scalar.activation(
                    out=ds_t(t), in_=ds_t(t), func=ACT.Sqrt, bias=q_of(t), scale=-1.0,
                )

        es = {}

        def new_e():
            e = epool.tile([P, NK], F32, name="e")
            return e[:]

        def do_E(u):
            for j in range(UT):
                t = u * UT + j
                e = e1[u][:, j, :] if u < HALF else new_e()
                nc.scalar.activation(
                    out=e, in_=ds_t(t), func=ACT.Exp, bias=dmin[:, t : t + 1], scale=-1.0,
                    accum_out=ssum[:, t : t + 1],
                )
                es[t] = e

        def do_H(u):
            t0 = u * UT
            for j in range(UT):
                t = t0 + j
                nc.vector.scalar_tensor_tensor(
                    out=ds_t(t), in0=ds_t(t), scalar=dmin[:, t : t + 1], in1=es[t],
                    op0=ALU.subtract, op1=ALU.mult, accum_out=ed[:, t : t + 1],
                )
                if j == 0 and u >= HALF:
                    do_S(u)

        def do_S(u):
            t0 = u * UT
            nc.vector.reciprocal(out=rs[:, t0 : t0 + UT], in_=ssum[:, t0 : t0 + UT])

        def do_N(u, on_scalar):
            for j in range(UT):
                t = u * UT + j
                if n_on_scalar(t) != on_scalar:
                    continue
                if on_scalar:
                    nc.scalar.activation(out=ds_t(t), in_=es[t], func=ACT.Copy, scale=rs[:, t : t + 1])
                else:
                    nc.vector.tensor_scalar_mul(out=ds_t(t), in0=es[t], scalar1=rs[:, t : t + 1])

        def do_NG(u):
            for j in range(UT):
                t = u * UT + j
                nc.gpsimd.tensor_scalar(
                    out=es[t], in0=es[t], scalar1=rs[:, t : t + 1], scalar2=1.0, op0=ALU.mult, op1=ALU.mult,
                )

        def do_dmin(lo, hi):
            a, b = lo * UT, (hi - TAIL) * UT
            nc.vector.tensor_add(out=qt[:, a:b], in0=qts[:, a:b], in1=qtv[:, a:b])
            nc.vector.tensor_sub(out=dm2[:, a:b], in0=qt[:, a:b], in1=um[:, a:b])
            nc.scalar.activation(out=dmin[:, a:b], in_=dm2[:, a:b], func=ACT.Sqrt)

        stores = [(u * UT, u * UT + UT) for u in range(HALF, NU - 1)] + [(NT - 2, NT - 1), (NT - 1, NT)]

        def n_step(t):
            return t // UT + (1 if n_on_scalar(t) else 0)

        def deferred(i):
            n = NU - HALF - TAIL
            if i >= n:
                return []
            return list(range(i * HALF // n, (i + 1) * HALF // n))

        t_tile(0)
        t_tile(1)
        t_tile(2)
        do_Q(0)
        do_Q(1)
        c_tile(0)
        quantise_p(3)
        t_tile(3)
        c_tile(1)
        ptp = build_pt_rows()
        c_tile(2)
        c_tile(3)
        do_T(2)
        do_Z(0)
        do_M(0)
        do_D(0)
        nc.vector.tensor_copy(out=pt[:], in_=ptp[:])

        for lo, hi in ((0, HALF), (HALF, NU)):
            first = lo == 0
            for s in range(lo, hi + 1):
                if s % 2 == 0 and 3 <= (s + 4) // 2 < NCH and s < hi:
                    load((s + 4) // 2)
                inner = s < hi
                if inner and s + 1 < NU:
                    do_Z(s + 1)
                    do_M(s + 1)
                for r in deferred(s - lo) if inner and not first else []:
                    do_S(r)
                    do_NG(r)
                if inner and s + 2 < NU and not (first and s == hi - 1):
                    do_C(s + 2, True)
                    if s + 3 < NU:
                        do_T(s + 3)
                    do_Q(s + 2)
                if inner:
                    do_A(s)
                    do_X(s)
                    if late(s):
                        do_KV(s)
                    elif first:
                        do_K(s)
                    else:
                        do_BV(s)
                if inner and s + 1 < NU:
                    do_D(s + 1)
                if first and s - 1 >= lo and not late(s - 1):
                    do_B(s - 1)
                if inner and s + 2 < NU and not (first and s == hi - 1):
                    do_C(s + 2, False)
                if first and s - 2 >= lo and not late(s - 2):
                    do_R(s - 2)
                if s - 1 >= lo and (late(s - 1) or not first):
                    do_R(s - 1)
                if s == hi - TAIL + 1:
                    do_dmin(lo, hi)
                for r in deferred(s - lo) if inner and not first else []:
                    nc.sync.dma_start(out=ov[:, r * UT : r * UT + UT, :], in_=e1[r][:])
            for u in range(hi - TAIL, hi):
                do_Bmin(u)
            for s in range(lo - 1, hi + 1):
                if lo <= s + 1 < hi:
                    do_E(s + 1)
                    if first and s + 1 == hi - 1:
                        do_C(hi + 1, True)
                        do_T(hi + 2)
                        do_Q(hi + 1)
                if lo <= s < hi:
                    do_H(s)
                    if not first:
                        do_N(s, False)
                if lo <= s - 1 < hi and not first:
                    do_N(s - 1, True)
                if first and s == hi:
                    do_C(hi + 1, False)
                if not first:
                    for a, b in stores:
                        if max(n_step(t) for t in range(a, b)) == s:
                            r = a - HALF * UT
                            nc.sync.dma_start(out=ov[:, a:b, :], in_=ds[r // CT][:, r % CT : r % CT + (b - a), :])

        nc.sync.dma_start(out=out_1.rearrange("(p t) -> p t", t=NT), in_=rs[:])
        nc.scalar.activation(out=lns[:], in_=ssum[:], func=ACT.Ln)
        nc.vector.tensor_mul(out=hh[:], in0=ed[:], in1=rs[:])
        nc.vector.tensor_add(out=hh[:], in0=hh[:], in1=lns[:])
        nc.sync.dma_start(out=out_2.rearrange("(p t) -> p t", t=NT), in_=hh[:])
